import numpy as np
import ml_dtypes


def mxq(x, axis, fmt="e4m3"):
    dtype, down = {"e4m3": (ml_dtypes.float8_e4m3fn, 7), "e5m2": (ml_dtypes.float8_e5m2, 14)}[fmt]
    v = np.moveaxis(np.asarray(x, np.float32).astype(ml_dtypes.bfloat16).astype(np.float64), axis, -1)
    blocks = v.reshape(v.shape[:-1] + (-1, 32))
    amax = np.abs(blocks).max(-1, keepdims=True)
    byte = np.maximum(np.where(amax > 0, np.frexp(amax)[1] - 1 + 127, 0) - down, 1)
    scale = np.exp2(byte - 127.0)
    codes = (blocks / scale).astype(np.float32).astype(dtype).astype(np.float64)
    return np.moveaxis((codes * scale).reshape(v.shape), -1, axis)


WIDE = False


def mx_kscale(k):
    if not WIDE:
        return np.ones(k)
    levels = np.array([10, -10, 5, -5, 0])
    a = np.random.permutation(np.resize(levels, k // 512 * 4)).reshape(k // 512, 4)
    idx = np.arange(k)
    return np.exp2(a[idx // 512, idx % 128 // 32])


BF16 = ml_dtypes.bfloat16


def bf(x):
    return np.asarray(x, np.float32).astype(BF16)


def f64(x):
    return np.asarray(x).astype(np.float64)


NB, D, CO, CV, R = 8, 256, 1024, 512, 512


def setup_inputs():
    s, t = mx_kscale(CV), mx_kscale(R)
    return {"x1": bf(np.random.standard_normal((NB, D, CO))),
            "A": bf(np.random.standard_normal((D, R)) / np.sqrt(D) * t),
            "t2": bf(np.random.standard_normal((NB, R, CV)) * s),
            "w": bf(np.random.standard_normal((NB, CO, CV)) / np.sqrt(CV) / s),
            "C": bf(np.random.standard_normal((D, R)) / np.sqrt(R) / t)}


def reference(x1, A, t2, w, C):
    t1 = f64(A).T @ f64(x1)
    t3 = mxq(f64(t2), 2, "e4m3") @ mxq(f64(w).transpose(0, 2, 1), 1, "e4m3")
    h = t1 * t3
    return mxq(f64(C), 1, "e4m3") @ mxq(h, 1, "e4m3")

@@ -1,0 +1,246 @@
+from contextlib import ExitStack
+
+import concourse.mybir as mybir
+from concourse.masks import make_identity
+
+BF16 = mybir.dt.bfloat16
+F32 = mybir.dt.float32
+U32 = mybir.dt.uint32
+U8 = mybir.dt.uint8
+FP8X4 = mybir.dt.float8_e4m3fn_x4
+MULT = mybir.AluOpType.mult
+
+NB, D, CO, CV, R = 8, 256, 1024, 512, 512
+FLOPS = 2 * NB * (R * CO * D + R * CO * CV + D * CO * R)
+
+P = 128
+PACK = 4
+PAIR = 2
+BANK = 512
+D_TILES = D // P
+CHUNKS = CO // P
+HALVES = CO // BANK
+BLOCK_ROWS = PACK * P
+W_BLOCKS = CO // BLOCK_ROWS
+CV_WORDS = CV // PAIR
+
+assert R == BLOCK_ROWS and CV == PACK * P and CV_WORDS == PAIR * P
+
+
+def tile_cptensorproduct_pa_t_kernel(tc, x1, A, t2, w, C, out):
+    nc = tc.nc
+    with ExitStack() as ctx:
+        const = ctx.enter_context(tc.tile_pool(name="const", bufs=1))
+        inputs = ctx.enter_context(tc.tile_pool(name="inputs", bufs=3))
+        staging = ctx.enter_context(tc.tile_pool(name="staging", bufs=3))
+        operands = ctx.enter_context(tc.tile_pool(name="operands", bufs=2))
+        t1_pool = ctx.enter_context(tc.tile_pool(name="t1_pool", bufs=CHUNKS + 4))
+        results = ctx.enter_context(tc.tile_pool(name="results", bufs=4))
+        psum = ctx.enter_context(tc.psum_pool(name="psum", bufs=2))
+        ctx.enter_context(tc.manual_schedule())
+
+        x1_of, rows_of = {}, {}
+        grouped_of = {}
+        codes_of, scales_of = {}, {}
+        t1_of = {}
+        h_of = {}
+
+        def load_sample(b):
+            if b >= NB:
+                return
+            x1_sb = inputs.tile([P, D_TILES, CO], BF16)
+            nc.sync.dma_start(out=x1_sb[:], in_=x1[b].rearrange("(k p) c -> p k c", p=P))
+            x1_of[b] = x1_sb
+            t2_sb = inputs.tile([P, PACK * CV], BF16)
+            nc.sync.dma_start(out=t2_sb[:], in_=t2[b].rearrange("(p t) c -> p (t c)", t=PACK))
+            rows_of[(b, 0)] = t2_sb[:].bitcast(F32).rearrange("p (g c) -> p g c", g=PACK)
+            w_sb = inputs.tile([P, CHUNKS * CV], BF16)
+            w_words = w_sb[:].bitcast(F32).rearrange("p (g c) -> p g c", g=CHUNKS)
+            for i in range(W_BLOCKS):
+                nc.sync.dma_start(
+                    out=w_sb[:, i * PACK * CV : (i + 1) * PACK * CV].rearrange("p (g c) -> p g c", g=PACK),
+                    in_=w[b, i * BLOCK_ROWS : (i + 1) * BLOCK_ROWS, :].rearrange("(g p) c -> p g c", p=P),
+                )
+                rows_of[(b, 1 + i)] = w_words[:, i * PACK : (i + 1) * PACK, :]
+
+        def transposes_to_bank(sources, grouped_words):
+            xt_bank = psum.tile([P, PAIR, PAIR * P], F32)
+            for u in range(PAIR):
+                for g in range(PAIR):
+                    nc.tensor.transpose(xt_bank[:, u, g * P : (g + 1) * P], sources[u][g], ident[:])
+            nc.scalar.copy(out=grouped_words, in_=xt_bank[:].rearrange("p u r -> p r u"))
+
+        def transpose_block(b, block):
+            if b >= NB:
+                return
+            rows = rows_of[(b, block)]
+            grouped = staging.tile([P, BLOCK_ROWS * PACK], BF16, align_bytes=64)
+            grouped_words = grouped[:].bitcast(F32).rearrange("p (r u) -> p r u", u=PAIR)
+            for i in range(PACK // PAIR):
+                transposes_to_bank(
+                    [[rows[:, PAIR * i + g, u * P : (u + 1) * P] for g in range(PAIR)] for u in range(PAIR)],
+                    grouped_words[:, i * PAIR * P : (i + 1) * PAIR * P, :],
+                )
+            grouped_of[(b, block)] = grouped
+
+        def quantise_block(b, block):
+            if b < 0 or b >= NB:
+                return
+            if block == 0:
+                t2_codes = operands.tile([P, R], U32, align_bytes=64)
+                t2_scales = operands.tile([P, R], U8, align_bytes=64)
+                codes_of[(b, "t2")], scales_of[(b, "t2")] = t2_codes, t2_scales
+            if block == 1:
+                w_codes = operands.tile([P, CO], U32, align_bytes=64)
+                w_scales = operands.tile([P, CO], U8, align_bytes=64)
+                codes_of[(b, "w")], scales_of[(b, "w")] = w_codes, w_scales
+            name = "t2" if block == 0 else "w"
+            first = 0 if block == 0 else (block - 1) * BLOCK_ROWS
+            cols = slice(first, first + BLOCK_ROWS)
+            nc.vector.quantize_mx(
+                out=codes_of[(b, name)][:, cols].bitcast(FP8X4),
+                scales=scales_of[(b, name)][:, cols],
+                in_=grouped_of[(b, block)][:],
+            )
+
+        def project_chunk(b, c):
+            if b >= NB:
+                return
+            t1_bank = psum.tile([P, PACK, P], F32)
+            for t in range(PACK):
+                for k in range(D_TILES):
+                    nc.tensor.matmul(
+                        t1_bank[:, t, :],
+                        lhsT=a_sorted[:, k, t, :],
+                        rhs=x1_of[b][:, k, c * P : (c + 1) * P],
+                        start=(k == 0),
+                        stop=(k == D_TILES - 1),
+                    )
+            t1_sb = t1_pool.tile([P, P, PACK], F32)
+            nc.scalar.copy(out=t1_sb[:], in_=t1_bank[:].rearrange("p t c -> p c t"))
+            t1_of[(b, c)] = t1_sb
+
+        def multiply_chunk(b, c):
+            if b < 0:
+                return
+            if c == 0:
+                h_grouped = operands.tile([P, CO * PACK], BF16, align_bytes=64)
+                h_of[b] = h_grouped
+            t3_bank = psum.tile([P, PACK, P], F32)
+            for t in range(PACK):
+                nc.tensor.matmul_mx(
+                    out=t3_bank[:, t, :],
+                    lhsT=codes_of[(b, "t2")][:, t * P : (t + 1) * P].bitcast(FP8X4),
+                    lhsT_scale=scales_of[(b, "t2")][:, t * P : (t + 1) * P],
+                    rhs=codes_of[(b, "w")][:, c * P : (c + 1) * P].bitcast(FP8X4),
+                    rhs_scale=scales_of[(b, "w")][:, c * P : (c + 1) * P],
+                    start=True,
+                    stop=True,
+                )
+            nc.vector.tensor_tensor(
+                out=h_of[b][:, c * P * PACK : (c + 1) * P * PACK].rearrange("p (c t) -> p c t", t=PACK),
+                in0=t3_bank[:].rearrange("p t c -> p c t"),
+                in1=t1_of[(b, c)][:],
+                op=MULT,
+            )
+
+        def quantise_h(b, half):
+            if b < 0:
+                return
+            if half == 0:
+                h_codes = operands.tile([P, CO], U32, align_bytes=64)
+                h_scales = operands.tile([P, CO], U8, align_bytes=64)
+                codes_of[(b, "h")], scales_of[(b, "h")] = h_codes, h_scales
+            cols = slice(half * BANK, (half + 1) * BANK)
+            nc.vector.quantize_mx(
+                out=codes_of[(b, "h")][:, cols].bitcast(FP8X4),
+                scales=scales_of[(b, "h")][:, cols],
+                in_=h_of[b][:, half * BANK * PACK : (half + 1) * BANK * PACK],
+            )
+
+        def output_half(b, half):
+            if b < 0:
+                return
+            cols = slice(half * BANK, (half + 1) * BANK)
+            for e in range(D_TILES):
+                out_bank = psum.tile([P, BANK], F32)
+                nc.tensor.matmul_mx(
+                    out=out_bank[:],
+                    lhsT=c_codes[:, e * P : (e + 1) * P].bitcast(FP8X4),
+                    lhsT_scale=c_scales[:, e * P : (e + 1) * P],
+                    rhs=codes_of[(b, "h")][:, cols].bitcast(FP8X4),
+                    rhs_scale=scales_of[(b, "h")][:, cols],
+                    start=True,
+                    stop=True,
+                )
+                out_sb = results.tile([P, BANK], F32)
+                if e == 0:
+                    nc.scalar.copy(out=out_sb[:], in_=out_bank[:])
+                else:
+                    nc.vector.tensor_copy(out=out_sb[:], in_=out_bank[:])
+                nc.sync.dma_start(out=out[b, e * P : (e + 1) * P, cols], in_=out_sb[:])
+
+        ident = const.tile([P, P], F32)
+        make_identity(nc, ident[:])
+        a_raw = const.tile([P, D_TILES, R], BF16)
+        nc.sync.dma_start(out=a_raw[:], in_=A.rearrange("(k p) r -> p k r", p=P))
+        c_raw = const.tile([P, D_TILES * R], BF16)
+        load_sample(0)
+        nc.sync.dma_start(
+            out=c_raw[:].rearrange("p (e r) -> p e r", e=D_TILES), in_=C.rearrange("(e p) r -> p e r", p=P)
+        )
+
+        a_sorted = const.tile([P, D_TILES, PACK, P], BF16)
+        nc.vector.tensor_copy(out=a_sorted[:], in_=a_raw[:].rearrange("p k (m t) -> p k t m", t=PACK))
+
+        def transpose_c():
+            c_words = c_raw[:].bitcast(F32).rearrange("p (e m u) -> p e u m", e=D_TILES, u=PAIR)
+            transposes_to_bank(
+                [[c_words[:, e, u, :] for e in range(D_TILES)] for u in range(PAIR)],
+                c_grouped[:].bitcast(F32).rearrange("p (r u) -> p r u", u=PAIR),
+            )
+
+        c_grouped = const.tile([P, D * PACK], BF16, align_bytes=64)
+        c_codes = const.tile([P, D], U32, align_bytes=64)
+        c_scales = const.tile([P, D], U8, align_bytes=64)
+
+        for b in range(-1, NB):
+            nxt = b + 1
+            load_sample(b + 2)
+
+            multiply_chunk(b, 0)
+            quantise_h(b - 1, 1)
+            quantise_block(b, 2)
+            project_chunk(nxt, 0)
+            if b == 0:
+                transpose_c()
+            project_chunk(nxt, 1)
+            multiply_chunk(b, 1)
+
+            multiply_chunk(b, 2)
+            output_half(b - 1, 1)
+            if b == 0:
+                nc.vector.quantize_mx(out=c_codes[:].bitcast(FP8X4), scales=c_scales[:], in_=c_grouped[:])
+            project_chunk(nxt, 2)
+            transpose_block(nxt, 0)
+            project_chunk(nxt, 3)
+            multiply_chunk(b, 3)
+
+            multiply_chunk(b, 4)
+            quantise_h(b, 0)
+            quantise_block(nxt, 0)
+            project_chunk(nxt, 4)
+            transpose_block(nxt, 1)
+            project_chunk(nxt, 5)
+            multiply_chunk(b, 5)
+
+            multiply_chunk(b, 6)
+            output_half(b, 0)
+            quantise_block(nxt, 1)
+            project_chunk(nxt, 6)
+            transpose_block(nxt, 2)
+            project_chunk(nxt, 7)
+            multiply_chunk(b, 7)
+
+        quantise_h(NB - 1, 1)
+        output_half(NB - 1, 1)

@@ -17,6 +17,7 @@ P = 128
 PACK = 4
 PAIR = 2
 BANK = 512
+PSUM_BANKS = 8
 D_TILES = D // P
 CHUNKS = CO // P
 HALVES = CO // BANK
@@ -36,7 +37,7 @@ def tile_cptensorproduct_pa_t_kernel(tc, x1, A, t2, w, C, out):
         operands = ctx.enter_context(tc.tile_pool(name="operands", bufs=2))
         t1_pool = ctx.enter_context(tc.tile_pool(name="t1_pool", bufs=CHUNKS + 4))
         results = ctx.enter_context(tc.tile_pool(name="results", bufs=4))
-        psum = ctx.enter_context(tc.psum_pool(name="psum", bufs=2))
+        psum = ctx.enter_context(tc.psum_pool(name="psum", bufs=PSUM_BANKS))
         ctx.enter_context(tc.manual_schedule())
 
         x1_of, rows_of = {}, {}
@@ -64,7 +65,7 @@ def tile_cptensorproduct_pa_t_kernel(tc, x1, A, t2, w, C, out):
                 rows_of[(b, 1 + i)] = w_words[:, i * PACK : (i + 1) * PACK, :]
 
         def transposes_to_bank(sources, grouped_words):
-            xt_bank = psum.tile([P, PAIR, PAIR * P], F32)
+            xt_bank = psum.tile([P, PAIR, PAIR * P], F32, tag="bank")
             for u in range(PAIR):
                 for g in range(PAIR):
                     nc.tensor.transpose(xt_bank[:, u, g * P : (g + 1) * P], sources[u][g], ident[:])
@@ -103,10 +104,11 @@ def tile_cptensorproduct_pa_t_kernel(tc, x1, A, t2, w, C, out):
                 in_=grouped_of[(b, block)][:],
             )
 
-        def project_chunk(b, c):
+        def project_next():
+            b, c = divmod(len(t1_of), CHUNKS)
             if b >= NB:
                 return
-            t1_bank = psum.tile([P, PACK, P], F32)
+            t1_bank = psum.tile([P, PACK, P], F32, tag="bank")
             for t in range(PACK):
                 for k in range(D_TILES):
                     nc.tensor.matmul(
@@ -126,7 +128,7 @@ def tile_cptensorproduct_pa_t_kernel(tc, x1, A, t2, w, C, out):
             if c == 0:
                 h_grouped = operands.tile([P, CO * PACK], BF16, align_bytes=64)
                 h_of[b] = h_grouped
-            t3_bank = psum.tile([P, PACK, P], F32)
+            t3_bank = psum.tile([P, PACK, P], F32, tag="bank")
             for t in range(PACK):
                 nc.tensor.matmul_mx(
                     out=t3_bank[:, t, :],
@@ -163,7 +165,7 @@ def tile_cptensorproduct_pa_t_kernel(tc, x1, A, t2, w, C, out):
                 return
             cols = slice(half * BANK, (half + 1) * BANK)
             for e in range(D_TILES):
-                out_bank = psum.tile([P, BANK], F32)
+                out_bank = psum.tile([P, BANK], F32, tag="bank")
                 nc.tensor.matmul_mx(
                     out=out_bank[:],
                     lhsT=c_codes[:, e * P : (e + 1) * P].bitcast(FP8X4),
@@ -204,42 +206,41 @@ def tile_cptensorproduct_pa_t_kernel(tc, x1, A, t2, w, C, out):
         c_codes = const.tile([P, D], U32, align_bytes=64)
         c_scales = const.tile([P, D], U8, align_bytes=64)
 
+        project_next()
         for b in range(-1, NB):
             nxt = b + 1
             load_sample(b + 2)
 
             multiply_chunk(b, 0)
             quantise_h(b - 1, 1)
-            quantise_block(b, 2)
-            project_chunk(nxt, 0)
-            if b == 0:
-                transpose_c()
-            project_chunk(nxt, 1)
+            project_next()
+            transpose_block(nxt, 0)
+            project_next()
             multiply_chunk(b, 1)
 
             multiply_chunk(b, 2)
-            output_half(b - 1, 1)
-            if b == 0:
-                nc.vector.quantize_mx(out=c_codes[:].bitcast(FP8X4), scales=c_scales[:], in_=c_grouped[:])
-            project_chunk(nxt, 2)
-            transpose_block(nxt, 0)
-            project_chunk(nxt, 3)
+            quantise_block(nxt, 0)
+            project_next()
+            transpose_block(nxt, 1)
+            project_next()
             multiply_chunk(b, 3)
 
             multiply_chunk(b, 4)
+            output_half(b - 1, 1)
             quantise_h(b, 0)
-            quantise_block(nxt, 0)
-            project_chunk(nxt, 4)
-            transpose_block(nxt, 1)
-            project_chunk(nxt, 5)
+            quantise_block(nxt, 1)
+            project_next()
+            transpose_block(nxt, 2)
+            project_next()
             multiply_chunk(b, 5)
 
             multiply_chunk(b, 6)
             output_half(b, 0)
-            quantise_block(nxt, 1)
-            project_chunk(nxt, 6)
-            transpose_block(nxt, 2)
-            project_chunk(nxt, 7)
+            quantise_block(nxt, 2)
+            if b < 0:
+                transpose_c()
+                nc.vector.quantize_mx(out=c_codes[:].bitcast(FP8X4), scales=c_scales[:], in_=c_grouped[:])
+            project_next()
             multiply_chunk(b, 7)
 
         quantise_h(NB - 1, 1)

@@ -20,12 +20,16 @@ BANK = 512
 PSUM_BANKS = 8
 D_TILES = D // P
 CHUNKS = CO // P
-HALVES = CO // BANK
+QUARTERS = 4
+QUARTER = CO // QUARTERS
 BLOCK_ROWS = PACK * P
 W_BLOCKS = CO // BLOCK_ROWS
+BLOCKS = 1 + W_BLOCKS
+OUTPUT_LAG = 2
 CV_WORDS = CV // PAIR
 
 assert R == BLOCK_ROWS and CV == PACK * P and CV_WORDS == PAIR * P
+assert PACK * P == BANK and D_TILES * QUARTER == BANK and PAIR * PAIR * P == BANK
 
 
 def tile_cptensorproduct_pa_t_kernel(tc, x1, A, t2, w, C, out):
@@ -85,7 +89,7 @@ def tile_cptensorproduct_pa_t_kernel(tc, x1, A, t2, w, C, out):
             grouped_of[(b, block)] = grouped
 
         def quantise_block(b, block):
-            if b < 0 or b >= NB:
+            if b < 0 or b >= NB or block < 0:
                 return
             if block == 0:
                 t2_codes = operands.tile([P, R], U32, align_bytes=64)
@@ -146,28 +150,30 @@ def tile_cptensorproduct_pa_t_kernel(tc, x1, A, t2, w, C, out):
                 op=MULT,
             )
 
-        def quantise_h(b, half):
+        def quantise_quarter(index):
+            b, q = divmod(index, QUARTERS)
             if b < 0:
                 return
-            if half == 0:
+            if q == 0:
                 h_codes = operands.tile([P, CO], U32, align_bytes=64)
                 h_scales = operands.tile([P, CO], U8, align_bytes=64)
                 codes_of[(b, "h")], scales_of[(b, "h")] = h_codes, h_scales
-            cols = slice(half * BANK, (half + 1) * BANK)
+            cols = slice(q * QUARTER, (q + 1) * QUARTER)
             nc.vector.quantize_mx(
                 out=codes_of[(b, "h")][:, cols].bitcast(FP8X4),
                 scales=scales_of[(b, "h")][:, cols],
-                in_=h_of[b][:, half * BANK * PACK : (half + 1) * BANK * PACK],
+                in_=h_of[b][:, q * QUARTER * PACK : (q + 1) * QUARTER * PACK],
             )
 
-        def output_half(b, half):
+        def output_quarter(index):
+            b, q = divmod(index, QUARTERS)
             if b < 0:
                 return
-            cols = slice(half * BANK, (half + 1) * BANK)
+            cols = slice(q * QUARTER, (q + 1) * QUARTER)
+            out_bank = psum.tile([P, D_TILES, QUARTER], F32, tag="bank")
             for e in range(D_TILES):
-                out_bank = psum.tile([P, BANK], F32, tag="bank")
                 nc.tensor.matmul_mx(
-                    out=out_bank[:],
+                    out=out_bank[:, e, :],
                     lhsT=c_codes[:, e * P : (e + 1) * P].bitcast(FP8X4),
                     lhsT_scale=c_scales[:, e * P : (e + 1) * P],
                     rhs=codes_of[(b, "h")][:, cols].bitcast(FP8X4),
@@ -175,12 +181,12 @@ def tile_cptensorproduct_pa_t_kernel(tc, x1, A, t2, w, C, out):
                     start=True,
                     stop=True,
                 )
-                out_sb = results.tile([P, BANK], F32)
-                if e == 0:
-                    nc.scalar.copy(out=out_sb[:], in_=out_bank[:])
-                else:
-                    nc.vector.tensor_copy(out=out_sb[:], in_=out_bank[:])
-                nc.sync.dma_start(out=out[b, e * P : (e + 1) * P, cols], in_=out_sb[:])
+            out_sb = results.tile([P, D_TILES, QUARTER], F32)
+            if q < QUARTERS - 1:
+                nc.scalar.copy(out=out_sb[:], in_=out_bank[:])
+            else:
+                nc.vector.tensor_copy(out=out_sb[:], in_=out_bank[:])
+            nc.sync.dma_start(out=out[b].rearrange("(e p) c -> p e c", p=P)[:, :, cols], in_=out_sb[:])
 
         ident = const.tile([P, P], F32)
         make_identity(nc, ident[:])
@@ -208,40 +214,24 @@ def tile_cptensorproduct_pa_t_kernel(tc, x1, A, t2, w, C, out):
 
         project_next()
         for b in range(-1, NB):
-            nxt = b + 1
             load_sample(b + 2)
+            for q in range(QUARTERS):
+                index = QUARTERS * b + q
+                multiply_chunk(b, 2 * q)
+                quantise_quarter(index - 1)
+                quantise_block(b + 1, q - 1)
+                if q < BLOCKS:
+                    project_next()
+                    transpose_block(b + 1, q)
+                elif b < 0:
+                    transpose_c()
+                    nc.vector.quantize_mx(out=c_codes[:].bitcast(FP8X4), scales=c_scales[:], in_=c_grouped[:])
+                project_next()
+                multiply_chunk(b, 2 * q + 1)
+                output_quarter(index - OUTPUT_LAG)
 
-            multiply_chunk(b, 0)
-            quantise_h(b - 1, 1)
-            project_next()
-            transpose_block(nxt, 0)
-            project_next()
-            multiply_chunk(b, 1)
-
-            multiply_chunk(b, 2)
-            quantise_block(nxt, 0)
-            project_next()
-            transpose_block(nxt, 1)
-            project_next()
-            multiply_chunk(b, 3)
-
-            multiply_chunk(b, 4)
-            output_half(b - 1, 1)
-            quantise_h(b, 0)
-            quantise_block(nxt, 1)
-            project_next()
-            transpose_block(nxt, 2)
-            project_next()
-            multiply_chunk(b, 5)
-
-            multiply_chunk(b, 6)
-            output_half(b, 0)
-            quantise_block(nxt, 2)
-            if b < 0:
-                transpose_c()
-                nc.vector.quantize_mx(out=c_codes[:].bitcast(FP8X4), scales=c_scales[:], in_=c_grouped[:])
-            project_next()
-            multiply_chunk(b, 7)
-
-        quantise_h(NB - 1, 1)
-        output_half(NB - 1, 1)
+        last = QUARTERS * NB - 1
+        for index in range(last - OUTPUT_LAG + 1, last):
+            output_quarter(index)
+        quantise_quarter(last)
+        output_quarter(last)

@@ -221,8 +221,8 @@ def tile_cptensorproduct_pa_t_kernel(tc, x1, A, t2, w, C, out):
                 quantise_quarter(index - 1)
                 quantise_block(b + 1, q - 1)
                 if q < BLOCKS:
-                    project_next()
                     transpose_block(b + 1, q)
+                    project_next()
                 elif b < 0:
                     transpose_c()
                     nc.vector.quantize_mx(out=c_codes[:].bitcast(FP8X4), scales=c_scales[:], in_=c_grouped[:])

@@ -18,6 +18,7 @@ PACK = 4
 PAIR = 2
 BANK = 512
 PSUM_BANKS = 8
+WARM_UPS = 8
 D_TILES = D // P
 CHUNKS = CO // P
 QUARTERS = 4
@@ -54,7 +55,10 @@ def tile_cptensorproduct_pa_t_kernel(tc, x1, A, t2, w, C, out):
             if b >= NB:
                 return
             x1_sb = inputs.tile([P, D_TILES, CO], BF16)
-            nc.sync.dma_start(out=x1_sb[:], in_=x1[b].rearrange("(k p) c -> p k c", p=P))
+            pieces = 2 if b == 0 else 1
+            for i in range(pieces):
+                cols = slice(i * CO // pieces, (i + 1) * CO // pieces)
+                nc.sync.dma_start(out=x1_sb[:, :, cols], in_=x1[b].rearrange("(k p) c -> p k c", p=P)[:, :, cols])
             x1_of[b] = x1_sb
             t2_sb = inputs.tile([P, PACK * CV], BF16)
             nc.sync.dma_start(out=t2_sb[:], in_=t2[b].rearrange("(p t) c -> p (t c)", t=PACK))
@@ -68,12 +72,12 @@ def tile_cptensorproduct_pa_t_kernel(tc, x1, A, t2, w, C, out):
                 )
                 rows_of[(b, 1 + i)] = w_words[:, i * PACK : (i + 1) * PACK, :]
 
-        def transposes_to_bank(sources, grouped_words):
+        def transposes_to_bank(sources, grouped_words, copy):
             xt_bank = psum.tile([P, PAIR, PAIR * P], F32, tag="bank")
             for u in range(PAIR):
                 for g in range(PAIR):
                     nc.tensor.transpose(xt_bank[:, u, g * P : (g + 1) * P], sources[u][g], ident[:])
-            nc.scalar.copy(out=grouped_words, in_=xt_bank[:].rearrange("p u r -> p r u"))
+            copy(out=grouped_words, in_=xt_bank[:].rearrange("p u r -> p r u"))
 
         def transpose_block(b, block):
             if b >= NB:
@@ -85,6 +89,7 @@ def tile_cptensorproduct_pa_t_kernel(tc, x1, A, t2, w, C, out):
                 transposes_to_bank(
                     [[rows[:, PAIR * i + g, u * P : (u + 1) * P] for g in range(PAIR)] for u in range(PAIR)],
                     grouped_words[:, i * PAIR * P : (i + 1) * PAIR * P, :],
+                    nc.vector.tensor_copy if b == 0 and i == 1 else nc.scalar.copy,
                 )
             grouped_of[(b, block)] = grouped
 
@@ -123,7 +128,8 @@ def tile_cptensorproduct_pa_t_kernel(tc, x1, A, t2, w, C, out):
                         stop=(k == D_TILES - 1),
                     )
             t1_sb = t1_pool.tile([P, P, PACK], F32)
-            nc.scalar.copy(out=t1_sb[:], in_=t1_bank[:].rearrange("p t c -> p c t"))
+            copy = nc.vector.tensor_copy if b == 0 and c % 2 == 1 else nc.scalar.copy
+            copy(out=t1_sb[:], in_=t1_bank[:].rearrange("p t c -> p c t"))
             t1_of[(b, c)] = t1_sb
 
         def multiply_chunk(b, c):
@@ -158,11 +164,13 @@ def tile_cptensorproduct_pa_t_kernel(tc, x1, A, t2, w, C, out):
                 h_codes = operands.tile([P, CO], U32, align_bytes=64)
                 h_scales = operands.tile([P, CO], U8, align_bytes=64)
                 codes_of[(b, "h")], scales_of[(b, "h")] = h_codes, h_scales
-            cols = slice(q * QUARTER, (q + 1) * QUARTER)
+            quantise_h(b, q * QUARTER, (q + 1) * QUARTER)
+
+        def quantise_h(b, first, end):
             nc.vector.quantize_mx(
-                out=codes_of[(b, "h")][:, cols].bitcast(FP8X4),
-                scales=scales_of[(b, "h")][:, cols],
-                in_=h_of[b][:, q * QUARTER * PACK : (q + 1) * QUARTER * PACK],
+                out=codes_of[(b, "h")][:, first:end].bitcast(FP8X4),
+                scales=scales_of[(b, "h")][:, first:end],
+                in_=h_of[b][:, first * PACK : end * PACK],
             )
 
         def output_quarter(index):
@@ -188,6 +196,30 @@ def tile_cptensorproduct_pa_t_kernel(tc, x1, A, t2, w, C, out):
                 nc.vector.tensor_copy(out=out_sb[:], in_=out_bank[:])
             nc.sync.dma_start(out=out[b].rearrange("(e p) c -> p e c", p=P)[:, :, cols], in_=out_sb[:])
 
+        def output_chunk(c):
+            b = NB - 1
+            cols = slice(c * P, (c + 1) * P)
+            for e in range(D_TILES):
+                out_bank = psum.tile([P, P], F32, tag="bank")
+                nc.tensor.matmul_mx(
+                    out=out_bank[:],
+                    lhsT=c_codes[:, e * P : (e + 1) * P].bitcast(FP8X4),
+                    lhsT_scale=c_scales[:, e * P : (e + 1) * P],
+                    rhs=codes_of[(b, "h")][:, cols].bitcast(FP8X4),
+                    rhs_scale=scales_of[(b, "h")][:, cols],
+                    start=True,
+                    stop=True,
+                )
+                piece_sb = results.tile([P, P], F32)
+                copy, queue = ((nc.scalar.copy, nc.scalar), (nc.vector.tensor_copy, nc.sync))[e]
+                copy(out=piece_sb[:], in_=out_bank[:])
+                queue.dma_start(out=out[b, e * P : (e + 1) * P, cols], in_=piece_sb[:])
+
+        zeros = const.tile([P, QUARTER], BF16)
+        nc.gpsimd.memset(zeros[:], 0.0)
+        warm_bank = psum.tile([P, QUARTER], F32, tag="bank")
+        for i in range(WARM_UPS):
+            nc.tensor.matmul(warm_bank[:], lhsT=zeros[:, 0:P], rhs=zeros[:], start=True, stop=True)
         ident = const.tile([P, P], F32)
         make_identity(nc, ident[:])
         a_raw = const.tile([P, D_TILES, R], BF16)
@@ -199,19 +231,22 @@ def tile_cptensorproduct_pa_t_kernel(tc, x1, A, t2, w, C, out):
         )
 
         a_sorted = const.tile([P, D_TILES, PACK, P], BF16)
-        nc.vector.tensor_copy(out=a_sorted[:], in_=a_raw[:].rearrange("p k (m t) -> p k t m", t=PACK))
+        for t in range(PACK):
+            nc.vector.tensor_copy(out=a_sorted[:, :, t, :], in_=a_raw[:].rearrange("p k (m t) -> p k t m", t=PACK)[:, :, t, :])
 
         def transpose_c():
             c_words = c_raw[:].bitcast(F32).rearrange("p (e m u) -> p e u m", e=D_TILES, u=PAIR)
             transposes_to_bank(
                 [[c_words[:, e, u, :] for e in range(D_TILES)] for u in range(PAIR)],
                 c_grouped[:].bitcast(F32).rearrange("p (r u) -> p r u", u=PAIR),
+                nc.scalar.copy,
             )
 
         c_grouped = const.tile([P, D * PACK], BF16, align_bytes=64)
         c_codes = const.tile([P, D], U32, align_bytes=64)
         c_scales = const.tile([P, D], U8, align_bytes=64)
 
+        project_next()
         project_next()
         for b in range(-1, NB):
             load_sample(b + 2)
@@ -226,12 +261,15 @@ def tile_cptensorproduct_pa_t_kernel(tc, x1, A, t2, w, C, out):
                 elif b < 0:
                     transpose_c()
                     nc.vector.quantize_mx(out=c_codes[:].bitcast(FP8X4), scales=c_scales[:], in_=c_grouped[:])
-                project_next()
+                if b >= 0 or q < QUARTERS - 1:
+                    project_next()
                 multiply_chunk(b, 2 * q + 1)
                 output_quarter(index - OUTPUT_LAG)
 
         last = QUARTERS * NB - 1
         for index in range(last - OUTPUT_LAG + 1, last):
             output_quarter(index)
-        quantise_quarter(last)
-        output_quarter(last)
+        for c in range(CHUNKS - 2, CHUNKS):
+            quantise_h(NB - 1, c * P, (c + 1) * P)
+        for c in range(CHUNKS - 2, CHUNKS):
+            output_chunk(c)

from contextlib import ExitStack

import concourse.mybir as mybir
from concourse.masks import make_identity

BF16 = mybir.dt.bfloat16
F32 = mybir.dt.float32
U32 = mybir.dt.uint32
U8 = mybir.dt.uint8
FP8X4 = mybir.dt.float8_e4m3fn_x4
MULT = mybir.AluOpType.mult

NB, D, CO, CV, R = 8, 256, 1024, 512, 512
FLOPS = 2 * NB * (R * CO * D + R * CO * CV + D * CO * R)

P = 128
PACK = 4
PAIR = 2
BANK = 512
PSUM_BANKS = 8
WARM_UPS = 8
D_TILES = D // P
CHUNKS = CO // P
QUARTERS = 4
QUARTER = CO // QUARTERS
BLOCK_ROWS = PACK * P
W_BLOCKS = CO // BLOCK_ROWS
BLOCKS = 1 + W_BLOCKS
OUTPUT_LAG = 2
CV_WORDS = CV // PAIR

assert R == BLOCK_ROWS and CV == PACK * P and CV_WORDS == PAIR * P
assert PACK * P == BANK and D_TILES * QUARTER == BANK and PAIR * PAIR * P == BANK


def tile_cptensorproduct_pa_t_kernel(tc, x1, A, t2, w, C, out):
    nc = tc.nc
    with ExitStack() as ctx:
        const = ctx.enter_context(tc.tile_pool(name="const", bufs=1))
        inputs = ctx.enter_context(tc.tile_pool(name="inputs", bufs=3))
        staging = ctx.enter_context(tc.tile_pool(name="staging", bufs=3))
        operands = ctx.enter_context(tc.tile_pool(name="operands", bufs=2))
        t1_pool = ctx.enter_context(tc.tile_pool(name="t1_pool", bufs=CHUNKS + 4))
        results = ctx.enter_context(tc.tile_pool(name="results", bufs=4))
        psum = ctx.enter_context(tc.psum_pool(name="psum", bufs=PSUM_BANKS))
        ctx.enter_context(tc.manual_schedule())

        x1_of, rows_of = {}, {}
        grouped_of = {}
        codes_of, scales_of = {}, {}
        t1_of = {}
        h_of = {}

        def load_sample(b):
            if b >= NB:
                return
            x1_sb = inputs.tile([P, D_TILES, CO], BF16)
            pieces = 2 if b == 0 else 1
            for i in range(pieces):
                cols = slice(i * CO // pieces, (i + 1) * CO // pieces)
                nc.sync.dma_start(out=x1_sb[:, :, cols], in_=x1[b].rearrange("(k p) c -> p k c", p=P)[:, :, cols])
            x1_of[b] = x1_sb
            t2_sb = inputs.tile([P, PACK * CV], BF16)
            nc.sync.dma_start(out=t2_sb[:], in_=t2[b].rearrange("(p t) c -> p (t c)", t=PACK))
            rows_of[(b, 0)] = t2_sb[:].bitcast(F32).rearrange("p (g c) -> p g c", g=PACK)
            w_sb = inputs.tile([P, CHUNKS * CV], BF16)
            w_words = w_sb[:].bitcast(F32).rearrange("p (g c) -> p g c", g=CHUNKS)
            for i in range(W_BLOCKS):
                nc.sync.dma_start(
                    out=w_sb[:, i * PACK * CV : (i + 1) * PACK * CV].rearrange("p (g c) -> p g c", g=PACK),
                    in_=w[b, i * BLOCK_ROWS : (i + 1) * BLOCK_ROWS, :].rearrange("(g p) c -> p g c", p=P),
                )
                rows_of[(b, 1 + i)] = w_words[:, i * PACK : (i + 1) * PACK, :]

        def transposes_to_bank(sources, grouped_words, copy):
            xt_bank = psum.tile([P, PAIR, PAIR * P], F32, tag="bank")
            for u in range(PAIR):
                for g in range(PAIR):
                    nc.tensor.transpose(xt_bank[:, u, g * P : (g + 1) * P], sources[u][g], ident[:])
            copy(out=grouped_words, in_=xt_bank[:].rearrange("p u r -> p r u"))

        def transpose_block(b, block):
            if b >= NB:
                return
            rows = rows_of[(b, block)]
            grouped = staging.tile([P, BLOCK_ROWS * PACK], BF16, align_bytes=64)
            grouped_words = grouped[:].bitcast(F32).rearrange("p (r u) -> p r u", u=PAIR)
            for i in range(PACK // PAIR):
                transposes_to_bank(
                    [[rows[:, PAIR * i + g, u * P : (u + 1) * P] for g in range(PAIR)] for u in range(PAIR)],
                    grouped_words[:, i * PAIR * P : (i + 1) * PAIR * P, :],
                    nc.vector.tensor_copy if b == 0 and i == 1 else nc.scalar.copy,
                )
            grouped_of[(b, block)] = grouped

        def quantise_block(b, block):
            if b < 0 or b >= NB or block < 0:
                return
            if block == 0:
                t2_codes = operands.tile([P, R], U32, align_bytes=64)
                t2_scales = operands.tile([P, R], U8, align_bytes=64)
                codes_of[(b, "t2")], scales_of[(b, "t2")] = t2_codes, t2_scales
            if block == 1:
                w_codes = operands.tile([P, CO], U32, align_bytes=64)
                w_scales = operands.tile([P, CO], U8, align_bytes=64)
                codes_of[(b, "w")], scales_of[(b, "w")] = w_codes, w_scales
            name = "t2" if block == 0 else "w"
            first = 0 if block == 0 else (block - 1) * BLOCK_ROWS
            cols = slice(first, first + BLOCK_ROWS)
            nc.vector.quantize_mx(
                out=codes_of[(b, name)][:, cols].bitcast(FP8X4),
                scales=scales_of[(b, name)][:, cols],
                in_=grouped_of[(b, block)][:],
            )

        def project_next():
            b, c = divmod(len(t1_of), CHUNKS)
            if b >= NB:
                return
            t1_bank = psum.tile([P, PACK, P], F32, tag="bank")
            for t in range(PACK):
                for k in range(D_TILES):
                    nc.tensor.matmul(
                        t1_bank[:, t, :],
                        lhsT=a_sorted[:, k, t, :],
                        rhs=x1_of[b][:, k, c * P : (c + 1) * P],
                        start=(k == 0),
                        stop=(k == D_TILES - 1),
                    )
            t1_sb = t1_pool.tile([P, P, PACK], F32)
            copy = nc.vector.tensor_copy if b == 0 and c % 2 == 1 else nc.scalar.copy
            copy(out=t1_sb[:], in_=t1_bank[:].rearrange("p t c -> p c t"))
            t1_of[(b, c)] = t1_sb

        def multiply_chunk(b, c):
            if b < 0:
                return
            if c == 0:
                h_grouped = operands.tile([P, CO * PACK], BF16, align_bytes=64)
                h_of[b] = h_grouped
            t3_bank = psum.tile([P, PACK, P], F32, tag="bank")
            for t in range(PACK):
                nc.tensor.matmul_mx(
                    out=t3_bank[:, t, :],
                    lhsT=codes_of[(b, "t2")][:, t * P : (t + 1) * P].bitcast(FP8X4),
                    lhsT_scale=scales_of[(b, "t2")][:, t * P : (t + 1) * P],
                    rhs=codes_of[(b, "w")][:, c * P : (c + 1) * P].bitcast(FP8X4),
                    rhs_scale=scales_of[(b, "w")][:, c * P : (c + 1) * P],
                    start=True,
                    stop=True,
                )
            nc.vector.tensor_tensor(
                out=h_of[b][:, c * P * PACK : (c + 1) * P * PACK].rearrange("p (c t) -> p c t", t=PACK),
                in0=t3_bank[:].rearrange("p t c -> p c t"),
                in1=t1_of[(b, c)][:],
                op=MULT,
            )

        def quantise_quarter(index):
            b, q = divmod(index, QUARTERS)
            if b < 0:
                return
            if q == 0:
                h_codes = operands.tile([P, CO], U32, align_bytes=64)
                h_scales = operands.tile([P, CO], U8, align_bytes=64)
                codes_of[(b, "h")], scales_of[(b, "h")] = h_codes, h_scales
            quantise_h(b, q * QUARTER, (q + 1) * QUARTER)

        def quantise_h(b, first, end):
            nc.vector.quantize_mx(
                out=codes_of[(b, "h")][:, first:end].bitcast(FP8X4),
                scales=scales_of[(b, "h")][:, first:end],
                in_=h_of[b][:, first * PACK : end * PACK],
            )

        def output_quarter(index):
            b, q = divmod(index, QUARTERS)
            if b < 0:
                return
            cols = slice(q * QUARTER, (q + 1) * QUARTER)
            out_bank = psum.tile([P, D_TILES, QUARTER], F32, tag="bank")
            for e in range(D_TILES):
                nc.tensor.matmul_mx(
                    out=out_bank[:, e, :],
                    lhsT=c_codes[:, e * P : (e + 1) * P].bitcast(FP8X4),
                    lhsT_scale=c_scales[:, e * P : (e + 1) * P],
                    rhs=codes_of[(b, "h")][:, cols].bitcast(FP8X4),
                    rhs_scale=scales_of[(b, "h")][:, cols],
                    start=True,
                    stop=True,
                )
            out_sb = results.tile([P, D_TILES, QUARTER], F32)
            if q < QUARTERS - 1:
                nc.scalar.copy(out=out_sb[:], in_=out_bank[:])
            else:
                nc.vector.tensor_copy(out=out_sb[:], in_=out_bank[:])
            nc.sync.dma_start(out=out[b].rearrange("(e p) c -> p e c", p=P)[:, :, cols], in_=out_sb[:])

        def output_chunk(c):
            b = NB - 1
            cols = slice(c * P, (c + 1) * P)
            for e in range(D_TILES):
                out_bank = psum.tile([P, P], F32, tag="bank")
                nc.tensor.matmul_mx(
                    out=out_bank[:],
                    lhsT=c_codes[:, e * P : (e + 1) * P].bitcast(FP8X4),
                    lhsT_scale=c_scales[:, e * P : (e + 1) * P],
                    rhs=codes_of[(b, "h")][:, cols].bitcast(FP8X4),
                    rhs_scale=scales_of[(b, "h")][:, cols],
                    start=True,
                    stop=True,
                )
                piece_sb = results.tile([P, P], F32)
                copy, queue = ((nc.scalar.copy, nc.scalar), (nc.vector.tensor_copy, nc.sync))[e]
                copy(out=piece_sb[:], in_=out_bank[:])
                queue.dma_start(out=out[b, e * P : (e + 1) * P, cols], in_=piece_sb[:])

        zeros = const.tile([P, QUARTER], BF16)
        nc.gpsimd.memset(zeros[:], 0.0)
        warm_bank = psum.tile([P, QUARTER], F32, tag="bank")
        for i in range(WARM_UPS):
            nc.tensor.matmul(warm_bank[:], lhsT=zeros[:, 0:P], rhs=zeros[:], start=True, stop=True)
        ident = const.tile([P, P], F32)
        make_identity(nc, ident[:])
        a_raw = const.tile([P, D_TILES, R], BF16)
        nc.sync.dma_start(out=a_raw[:], in_=A.rearrange("(k p) r -> p k r", p=P))
        c_raw = const.tile([P, D_TILES * R], BF16)
        load_sample(0)
        nc.sync.dma_start(
            out=c_raw[:].rearrange("p (e r) -> p e r", e=D_TILES), in_=C.rearrange("(e p) r -> p e r", p=P)
        )

        a_sorted = const.tile([P, D_TILES, PACK, P], BF16)
        for t in range(PACK):
            nc.vector.tensor_copy(out=a_sorted[:, :, t, :], in_=a_raw[:].rearrange("p k (m t) -> p k t m", t=PACK)[:, :, t, :])

        def transpose_c():
            c_words = c_raw[:].bitcast(F32).rearrange("p (e m u) -> p e u m", e=D_TILES, u=PAIR)
            transposes_to_bank(
                [[c_words[:, e, u, :] for e in range(D_TILES)] for u in range(PAIR)],
                c_grouped[:].bitcast(F32).rearrange("p (r u) -> p r u", u=PAIR),
                nc.scalar.copy,
            )

        c_grouped = const.tile([P, D * PACK], BF16, align_bytes=64)
        c_codes = const.tile([P, D], U32, align_bytes=64)
        c_scales = const.tile([P, D], U8, align_bytes=64)

        project_next()
        project_next()
        for b in range(-1, NB):
            load_sample(b + 2)
            for q in range(QUARTERS):
                index = QUARTERS * b + q
                multiply_chunk(b, 2 * q)
                quantise_quarter(index - 1)
                quantise_block(b + 1, q - 1)
                if q < BLOCKS:
                    transpose_block(b + 1, q)
                    project_next()
                elif b < 0:
                    transpose_c()
                    nc.vector.quantize_mx(out=c_codes[:].bitcast(FP8X4), scales=c_scales[:], in_=c_grouped[:])
                if b >= 0 or q < QUARTERS - 1:
                    project_next()
                multiply_chunk(b, 2 * q + 1)
                output_quarter(index - OUTPUT_LAG)

        last = QUARTERS * NB - 1
        for index in range(last - OUTPUT_LAG + 1, last):
            output_quarter(index)
        for c in range(CHUNKS - 2, CHUNKS):
            quantise_h(NB - 1, c * P, (c + 1) * P)
        for c in range(CHUNKS - 2, CHUNKS):
            output_chunk(c)
